import numpy as np
import ml_dtypes


def mxq(x, axis, fmt="e4m3"):
    dtype, down = {"e4m3": (ml_dtypes.float8_e4m3fn, 7), "e5m2": (ml_dtypes.float8_e5m2, 14)}[fmt]
    v = np.moveaxis(np.asarray(x, np.float32).astype(ml_dtypes.bfloat16).astype(np.float64), axis, -1)
    blocks = v.reshape(v.shape[:-1] + (-1, 32))
    amax = np.abs(blocks).max(-1, keepdims=True)
    byte = np.maximum(np.where(amax > 0, np.frexp(amax)[1] - 1 + 127, 0) - down, 1)
    scale = np.exp2(byte - 127.0)
    codes = (blocks / scale).astype(np.float32).astype(dtype).astype(np.float64)
    return np.moveaxis((codes * scale).reshape(v.shape), -1, axis)


WIDE = False


def mx_kscale(k):
    if not WIDE:
        return np.ones(k)
    levels = np.array([10, -10, 5, -5, 0])
    if k % 512:
        return np.exp2(np.random.permutation(np.resize(levels, k // 32))).repeat(32)
    a = np.empty((k // 512, 16))
    for p in range(k // 512):
        a[p, :8] = np.random.permutation(np.resize(levels, 8))
        for g in range(8):
            far = levels[np.abs(levels - a[p, g]) >= 10]
            a[p, g + 8] = far[np.random.randint(len(far))]
    return np.exp2(a.ravel()).repeat(32)


BF16 = ml_dtypes.bfloat16


def bf(x):
    return np.asarray(x, np.float32).astype(BF16)


def f64(x):
    return np.asarray(x).astype(np.float64)


B, I, H = 128, 256, 256
K = H + I
NAMES = ["w_f_light", "w_i_light", "w_c_light", "w_o_light",
         "w_f_light_temp", "w_i_light_temp", "w_c_light_temp", "w_o_light_temp"]


def sigmoid(v):
    return 1.0 / (1.0 + np.exp(-v))


def setup_inputs():
    s = mx_kscale(K)
    inp = {
        "y": bf(np.random.standard_normal((B, I)) * s[H:]),
        "h_light": bf(np.random.standard_normal((B, H)) * s[:H]),
        "c_light": bf(np.random.standard_normal((B, H))),
        "h_temp": bf(np.random.standard_normal((B, H)) * s[:H]),
        "c_temp": bf(np.random.standard_normal((B, H))),
    }
    for n in NAMES:
        inp[n] = bf(np.random.standard_normal((H, K)) / np.sqrt(K) / s)
        inp["b" + n[1:]] = bf(np.random.standard_normal(H) * 0.5)
    return inp


def _branch(hx, wf, b_f, wi, b_i, wc, b_c, wo, b_o):
    W = np.concatenate([wf, wi, wc, wo], axis=0)
    b = np.concatenate([b_f, b_i, b_c, b_o], axis=0)
    z = (mxq(hx, 1, "e4m3") @ mxq(W.T, 0, "e4m3")) + b
    zf, zi, zc, zo = np.split(z, 4, axis=1)
    return sigmoid(zf), sigmoid(zi), np.tanh(zc), sigmoid(zo)


def reference(y, h_light, c_light, h_temp, c_temp,
              w_f_light, b_f_light, w_i_light, b_i_light,
              w_c_light, b_c_light, w_o_light, b_o_light,
              w_f_light_temp, b_f_light_temp, w_i_light_temp, b_i_light_temp,
              w_c_light_temp, b_c_light_temp, w_o_light_temp, b_o_light_temp):
    y, h_light, c_light, h_temp = f64(y), f64(h_light), f64(c_light), f64(h_temp)
    hx_l = np.concatenate([h_light, y], axis=1)
    hx_t = np.concatenate([h_temp, y], axis=1)
    f1, i1, ch1, o1 = _branch(hx_l, f64(w_f_light), f64(b_f_light), f64(w_i_light), f64(b_i_light),
                              f64(w_c_light), f64(b_c_light), f64(w_o_light), f64(b_o_light))
    f2, i2, ch2, o2 = _branch(hx_t, f64(w_f_light_temp), f64(b_f_light_temp), f64(w_i_light_temp), f64(b_i_light_temp),
                              f64(w_c_light_temp), f64(b_c_light_temp), f64(w_o_light_temp), f64(b_o_light_temp))
    c_new = (f1 * c_light + i1 * ch1) + (f2 * c_light + i2 * ch2)
    h_new = (o1 + o2) * np.tanh(c_new)
    return h_new, c_new

@@ -1,0 +1,307 @@
+from contextlib import ExitStack
+
+import concourse.mybir as mybir
+from concourse.masks import make_identity
+
+BF16 = mybir.dt.bfloat16
+F32 = mybir.dt.float32
+U32 = mybir.dt.uint32
+U8 = mybir.dt.uint8
+FP8X4 = mybir.dt.float8_e4m3fn_x4
+ACT = mybir.ActivationFunctionType
+
+P = 128
+H = 256
+K = 2 * H
+BRANCHES = 2
+PARITIES = 2
+IDLE_AT_START = 10
+IDLE_ALONE = 6
+IDLE_BEHIND_A_GATE = 2
+GATES = ("i", "c", "f", "o")
+GATE_FUNC = {"i": ACT.Sigmoid, "c": ACT.Tanh, "f": ACT.Sigmoid, "o": ACT.Sigmoid}
+
+FLOPS = 2 * P * K * len(GATES) * BRANCHES * H
+
+
+def tile_customlstmcell_s_kernel(
+    tc,
+    y,
+    h_light,
+    c_light,
+    h_temp,
+    c_temp,
+    w_f_light,
+    b_f_light,
+    w_i_light,
+    b_i_light,
+    w_c_light,
+    b_c_light,
+    w_o_light,
+    b_o_light,
+    w_f_light_temp,
+    b_f_light_temp,
+    w_i_light_temp,
+    b_i_light_temp,
+    w_c_light_temp,
+    b_c_light_temp,
+    w_o_light_temp,
+    b_o_light_temp,
+    out_0,
+    out_1,
+):
+    nc = tc.nc
+    weight_of = {
+        "f": (w_f_light, w_f_light_temp),
+        "i": (w_i_light, w_i_light_temp),
+        "c": (w_c_light, w_c_light_temp),
+        "o": (w_o_light, w_o_light_temp),
+    }
+    bias_of = {
+        "f": (b_f_light, b_f_light_temp),
+        "i": (b_i_light, b_i_light_temp),
+        "c": (b_c_light, b_c_light_temp),
+        "o": (b_o_light, b_o_light_temp),
+    }
+
+    with ExitStack() as ctx:
+        keep = ctx.enter_context(tc.tile_pool(name="keep", bufs=1))
+        flipped = ctx.enter_context(tc.psum_pool(name="flipped", bufs=4))
+        sums = ctx.enter_context(tc.psum_pool(name="sums", bufs=2))
+        totals = ctx.enter_context(tc.psum_pool(name="totals", bufs=1))
+        ctx.enter_context(tc.manual_schedule())
+
+        c_total = totals.tile([P, H], F32, name="c_total")
+        o_total = totals.tile([P, H], F32, name="o_total")
+        zeros = keep.tile([P, 4 * P], BF16, name="zeros", align_bytes=64)
+        zero_codes = keep.tile([P, P], U32, name="zero_codes", align_bytes=64)
+        zero_scales = keep.tile([P, P], U8, name="zero_scales", align_bytes=64)
+        nc.vector.memset(zeros[:], 0.0)
+        nc.vector.quantize_mx(out=zero_codes[:].bitcast(FP8X4), scales=zero_scales[:], in_=zeros[:])
+
+        def idle_passes(count):
+            for repeat in range(count):
+                nc.tensor.matmul_mx(
+                    out=o_total[:, 0:P],
+                    lhsT=zero_codes[:].bitcast(FP8X4),
+                    lhsT_scale=zero_scales[:],
+                    rhs=zero_codes[:].bitcast(FP8X4),
+                    rhs_scale=zero_scales[:],
+                    start=True,
+                    stop=True,
+                )
+
+        idle_passes(IDLE_AT_START)
+
+        ident = keep.tile([P, P], F32, name="ident")
+        make_identity(nc, ident[:])
+        bias_rows = [keep.tile([P, H], BF16, name="bias_rows_%d" % half) for half in range(2)]
+        for half in range(2):
+            nc.vector.memset(bias_rows[half][:], 0.0)
+        warm_in = keep.tile([P, 1], F32, name="warm_in")
+        warm_out = keep.tile([P, 1], F32, name="warm_out")
+        nc.vector.memset(warm_in[:], 0.0)
+        nc.scalar.activation(out=warm_out[:], in_=warm_in[:], func=ACT.Sigmoid)
+
+        hx_sb = [keep.tile([P, K], BF16, name="hx_sb%d" % branch) for branch in range(BRANCHES)]
+        cl_sb = keep.tile([P, H], BF16, name="cl_sb")
+        w_sb = {}
+        for gate in GATES:
+            for branch in range(BRANCHES):
+                w_sb[gate, branch] = keep.tile([P, PARITIES * K], BF16, name="w_%s%d" % (gate, branch))
+
+        def load_weights(gate):
+            for branch in range(BRANCHES):
+                nc.sync.dma_start(
+                    out=w_sb[gate, branch][:],
+                    in_=weight_of[gate][branch].rearrange("(m a) k -> m (a k)", a=PARITIES),
+                )
+
+        def load_biases(half):
+            for place, gate in enumerate(GATES[2 * half : 2 * half + 2]):
+                for branch in range(BRANCHES):
+                    row = BRANCHES * place + branch
+                    nc.sync.dma_start(
+                        out=bias_rows[half][row : row + 1, :],
+                        in_=bias_of[gate][branch].rearrange("(o n) -> o n", o=1),
+                    )
+
+        nc.sync.dma_start(out=hx_sb[0][:, H:K], in_=y)
+        nc.sync.dma_start(out=hx_sb[0][:, 0:H], in_=h_light)
+        nc.sync.dma_start(out=hx_sb[1][:, 0:H], in_=h_temp)
+        nc.vector.tensor_copy(out=hx_sb[1][:, H:K], in_=hx_sb[0][:, H:K])
+        load_weights("i")
+        load_weights("c")
+        load_biases(0)
+        load_weights("f")
+        load_weights("o")
+        load_biases(1)
+        nc.sync.dma_start(out=cl_sb[:], in_=c_light)
+
+        def words(tile_bf16, first_word, step=1):
+            return tile_bf16[:].bitcast(F32)[:, first_word : first_word + (P - 1) * step + 1 : step]
+
+        def flip(*sources):
+            bank = flipped.tile([P, 2 * P], F32, name="bank", tag="bank")
+            for u, source in enumerate(sources):
+                nc.tensor.transpose(bank[:, u * P : (u + 1) * P], source, ident[:])
+            return bank
+
+        def quantise(second, bank, codes, scales, name):
+            grouped = keep.tile([P, 4 * P], BF16, name=name, align_bytes=64)
+            src = bank[:].rearrange("q (u r) -> q r u", u=2)
+            dst = grouped[:].bitcast(F32).rearrange("q (r u) -> q r u", u=2)
+            if second:
+                nc.vector.tensor_copy(out=dst, in_=src)
+            else:
+                nc.scalar.copy(out=dst, in_=src)
+            return lambda: nc.vector.quantize_mx(out=codes.bitcast(FP8X4), scales=scales, in_=grouped[:])
+
+        def halves(pair_of_sources, codes, scales, name):
+            pending = []
+            for second, sources in enumerate(pair_of_sources):
+                cols = slice(second * P, (second + 1) * P)
+                bank = flip(*sources)
+                pending.append(quantise(second, bank, codes[:, cols], scales[:, cols], "%s%d" % (name, second)))
+            for issue in pending:
+                issue()
+
+        hx_codes = keep.tile([P, BRANCHES * P], U32, name="hx_codes", align_bytes=64)
+        hx_scales = keep.tile([P, BRANCHES * P], U8, name="hx_scales", align_bytes=64)
+        halves(
+            [(words(hx_sb[branch], 0, 2), words(hx_sb[branch], 1, 2)) for branch in range(BRANCHES)],
+            hx_codes[:],
+            hx_scales[:],
+            "hx_grouped",
+        )
+
+        w_codes = keep.tile([P, len(GATES) * BRANCHES, H], U32, name="w_codes", align_bytes=64)
+        w_scales = keep.tile([P, len(GATES) * BRANCHES, H], U8, name="w_scales", align_bytes=64)
+        bias = keep.tile([P, len(GATES) * BRANCHES * PARITIES], F32, name="bias")
+        gate_sb = {}
+        for gate in GATES:
+            gate_sb[gate] = keep.tile([P, BRANCHES * H], F32, name="gate_%s" % gate)
+        z = {}
+
+        def slot_of(gate, branch):
+            return BRANCHES * GATES.index(gate) + branch
+
+        def prepare(gate, branch):
+            tile_bf16 = w_sb[gate, branch]
+            slot = slot_of(gate, branch)
+            halves(
+                [(words(tile_bf16, parity * H, 2), words(tile_bf16, parity * H + 1, 2)) for parity in range(PARITIES)],
+                w_codes[:, slot, :],
+                w_scales[:, slot, :],
+                "grouped_%s%d" % (gate, branch),
+            )
+
+        def flip_biases(half):
+            bank = flip(words(bias_rows[half], 0))
+            nc.scalar.copy(out=bias[:, 8 * half : 8 * half + 8], in_=bank[:, 0:4].bitcast(BF16))
+
+        def passes(gate, branch):
+            slot = slot_of(gate, branch)
+            z[gate, branch] = sums.tile([P, H], F32, name="z", tag="z")
+            for parity in range(PARITIES):
+                cols = slice(parity * P, (parity + 1) * P)
+                nc.tensor.matmul_mx(
+                    out=z[gate, branch][:, cols],
+                    lhsT=w_codes[:, slot, cols].bitcast(FP8X4),
+                    lhsT_scale=w_scales[:, slot, cols],
+                    rhs=hx_codes[:, branch * P : (branch + 1) * P].bitcast(FP8X4),
+                    rhs_scale=hx_scales[:, branch * P : (branch + 1) * P],
+                    start=True,
+                    stop=True,
+                )
+
+        def activate(gate, branch):
+            for parity in range(PARITIES):
+                column = PARITIES * slot_of(gate, branch) + parity
+                nc.scalar.activation(
+                    out=gate_sb[gate][:, branch * H + parity * P : branch * H + (parity + 1) * P],
+                    in_=z[gate, branch][:, parity * P : (parity + 1) * P],
+                    func=GATE_FUNC[gate],
+                    bias=bias[:, column : column + 1],
+                )
+
+        def add_transposed(total, terms, first, last):
+            for branch in range(BRANCHES):
+                for parity in range(PARITIES):
+                    nc.tensor.matmul(
+                        out=total[:, parity * P : (parity + 1) * P],
+                        lhsT=terms[:, branch * H + parity * P : branch * H + (parity + 1) * P],
+                        rhs=ident[:],
+                        start=first and branch == 0 and parity == 0,
+                        stop=last and branch == BRANCHES - 1 and parity == PARITIES - 1,
+                        is_transpose=True,
+                    )
+
+        for branch in range(BRANCHES):
+            prepare("i", branch)
+        idle_passes(IDLE_ALONE)
+        for branch in range(BRANCHES):
+            prepare("c", branch)
+        flip_biases(0)
+        for branch in range(BRANCHES):
+            passes("i", branch)
+        idle_passes(IDLE_BEHIND_A_GATE)
+        for branch in range(BRANCHES):
+            activate("i", branch)
+
+        for branch in range(BRANCHES):
+            prepare("f", branch)
+        for branch in range(BRANCHES):
+            passes("c", branch)
+        idle_passes(IDLE_BEHIND_A_GATE)
+        for branch in range(BRANCHES):
+            activate("c", branch)
+
+        prepare("o", 0)
+        written = keep.tile([P, BRANCHES * H], F32, name="written")
+        nc.vector.tensor_mul(out=written[:], in0=gate_sb["i"][:], in1=gate_sb["c"][:])
+        prepare("o", 1)
+        flip_biases(1)
+        cl_bank = flip(words(cl_sb, 0))
+        c_old = keep.tile([P, H], F32, name="c_old")
+        nc.scalar.copy(
+            out=c_old[:].rearrange("m (a b) -> m a b", a=PARITIES),
+            in_=cl_bank[:, 0:P].bitcast(BF16).rearrange("m (b a) -> m a b", a=PARITIES),
+        )
+        for branch in range(BRANCHES):
+            passes("f", branch)
+        idle_passes(IDLE_BEHIND_A_GATE)
+        for branch in range(BRANCHES):
+            activate("f", branch)
+        add_transposed(c_total, written, True, False)
+        kept = keep.tile([P, BRANCHES * H], F32, name="kept")
+        nc.vector.tensor_mul(
+            out=kept[:].rearrange("m (r n) -> m r n", r=BRANCHES),
+            in0=gate_sb["f"][:].rearrange("m (r n) -> m r n", r=BRANCHES),
+            in1=c_old[:].unsqueeze(1).to_broadcast([P, BRANCHES, H]),
+        )
+        for branch in range(BRANCHES):
+            passes("o", branch)
+            activate("o", branch)
+        add_transposed(c_total, kept, False, True)
+
+        tanh_c = keep.tile([P, H], F32, name="tanh_c")
+        nc.scalar.activation(
+            out=tanh_c[:].rearrange("b (m a) -> b m a", a=PARITIES),
+            in_=c_total[:].rearrange("b (a m) -> b m a", a=PARITIES),
+            func=ACT.Tanh,
+        )
+        c_rows = keep.tile([P, H], F32, name="c_rows")
+        nc.scalar.copy(
+            out=c_rows[:].rearrange("b (m a) -> b m a", a=PARITIES),
+            in_=c_total[:].rearrange("b (a m) -> b m a", a=PARITIES),
+        )
+        nc.sync.dma_start(out=out_1, in_=c_rows[:])
+        add_transposed(o_total, gate_sb["o"], True, True)
+        h_rows = keep.tile([P, H], F32, name="h_rows")
+        nc.vector.tensor_mul(
+            out=h_rows[:].rearrange("b (m a) -> b m a", a=PARITIES),
+            in0=o_total[:].rearrange("b (a m) -> b m a", a=PARITIES),
+            in1=tanh_c[:].rearrange("b (m a) -> b m a", a=PARITIES),
+        )
+        nc.sync.dma_start(out=out_0, in_=h_rows[:])

@@ -71,7 +71,7 @@ def tile_customlstmcell_s_kernel(
         totals = ctx.enter_context(tc.psum_pool(name="totals", bufs=1))
         ctx.enter_context(tc.manual_schedule())
 
-        c_total = totals.tile([P, H], F32, name="c_total")
+        c_total = totals.tile([P, 2 * H], F32, name="c_total")
         o_total = totals.tile([P, H], F32, name="o_total")
         zeros = keep.tile([P, 4 * P], BF16, name="zeros", align_bytes=64)
         zero_codes = keep.tile([P, P], U32, name="zero_codes", align_bytes=64)
@@ -95,9 +95,6 @@ def tile_customlstmcell_s_kernel(
 
         ident = keep.tile([P, P], F32, name="ident")
         make_identity(nc, ident[:])
-        bias_rows = [keep.tile([P, H], BF16, name="bias_rows_%d" % half) for half in range(2)]
-        for half in range(2):
-            nc.vector.memset(bias_rows[half][:], 0.0)
         warm_in = keep.tile([P, 1], F32, name="warm_in")
         warm_out = keep.tile([P, 1], F32, name="warm_out")
         nc.vector.memset(warm_in[:], 0.0)
@@ -110,6 +107,11 @@ def tile_customlstmcell_s_kernel(
             for branch in range(BRANCHES):
                 w_sb[gate, branch] = keep.tile([P, PARITIES * K], BF16, name="w_%s%d" % (gate, branch))
 
+        bias = keep.tile([P, len(GATES) * BRANCHES, 16], BF16, name="bias")
+
+        def slot_of(gate, branch):
+            return BRANCHES * GATES.index(gate) + branch
+
         def load_weights(gate):
             for branch in range(BRANCHES):
                 nc.sync.dma_start(
@@ -118,12 +120,11 @@ def tile_customlstmcell_s_kernel(
                 )
 
         def load_biases(half):
-            for place, gate in enumerate(GATES[2 * half : 2 * half + 2]):
+            for gate in GATES[2 * half : 2 * half + 2]:
                 for branch in range(BRANCHES):
-                    row = BRANCHES * place + branch
                     nc.sync.dma_start(
-                        out=bias_rows[half][row : row + 1, :],
-                        in_=bias_of[gate][branch].rearrange("(o n) -> o n", o=1),
+                        out=bias[:, slot_of(gate, branch), 0:PARITIES],
+                        in_=bias_of[gate][branch].rearrange("(m a) -> m a", a=PARITIES),
                     )
 
         nc.sync.dma_start(out=hx_sb[0][:, H:K], in_=y)
@@ -177,14 +178,10 @@ def tile_customlstmcell_s_kernel(
 
         w_codes = keep.tile([P, len(GATES) * BRANCHES, H], U32, name="w_codes", align_bytes=64)
         w_scales = keep.tile([P, len(GATES) * BRANCHES, H], U8, name="w_scales", align_bytes=64)
-        bias = keep.tile([P, len(GATES) * BRANCHES * PARITIES], F32, name="bias")
         gate_sb = {}
         for gate in GATES:
             gate_sb[gate] = keep.tile([P, BRANCHES * H], F32, name="gate_%s" % gate)
         z = {}
-
-        def slot_of(gate, branch):
-            return BRANCHES * GATES.index(gate) + branch
 
         def prepare(gate, branch):
             tile_bf16 = w_sb[gate, branch]
@@ -195,10 +192,6 @@ def tile_customlstmcell_s_kernel(
                 w_scales[:, slot, :],
                 "grouped_%s%d" % (gate, branch),
             )
-
-        def flip_biases(half):
-            bank = flip(words(bias_rows[half], 0))
-            nc.scalar.copy(out=bias[:, 8 * half : 8 * half + 8], in_=bank[:, 0:4].bitcast(BF16))
 
         def passes(gate, branch):
             slot = slot_of(gate, branch)
@@ -217,23 +210,22 @@ def tile_customlstmcell_s_kernel(
 
         def activate(gate, branch):
             for parity in range(PARITIES):
-                column = PARITIES * slot_of(gate, branch) + parity
                 nc.scalar.activation(
                     out=gate_sb[gate][:, branch * H + parity * P : branch * H + (parity + 1) * P],
                     in_=z[gate, branch][:, parity * P : (parity + 1) * P],
                     func=GATE_FUNC[gate],
-                    bias=bias[:, column : column + 1],
+                    bias=bias[:, slot_of(gate, branch), parity : parity + 1],
                 )
 
-        def add_transposed(total, terms, first, last):
+        def add_transposed(total, terms):
             for branch in range(BRANCHES):
                 for parity in range(PARITIES):
                     nc.tensor.matmul(
                         out=total[:, parity * P : (parity + 1) * P],
                         lhsT=terms[:, branch * H + parity * P : branch * H + (parity + 1) * P],
                         rhs=ident[:],
-                        start=first and branch == 0 and parity == 0,
-                        stop=last and branch == BRANCHES - 1 and parity == PARITIES - 1,
+                        start=branch == 0 and parity == 0,
+                        stop=branch == BRANCHES - 1 and parity == PARITIES - 1,
                         is_transpose=True,
                     )
 
@@ -242,7 +234,6 @@ def tile_customlstmcell_s_kernel(
         idle_passes(IDLE_ALONE)
         for branch in range(BRANCHES):
             prepare("c", branch)
-        flip_biases(0)
         for branch in range(BRANCHES):
             passes("i", branch)
         idle_passes(IDLE_BEHIND_A_GATE)
@@ -261,47 +252,31 @@ def tile_customlstmcell_s_kernel(
         written = keep.tile([P, BRANCHES * H], F32, name="written")
         nc.vector.tensor_mul(out=written[:], in0=gate_sb["i"][:], in1=gate_sb["c"][:])
         prepare("o", 1)
-        flip_biases(1)
-        cl_bank = flip(words(cl_sb, 0))
-        c_old = keep.tile([P, H], F32, name="c_old")
-        nc.scalar.copy(
-            out=c_old[:].rearrange("m (a b) -> m a b", a=PARITIES),
-            in_=cl_bank[:, 0:P].bitcast(BF16).rearrange("m (b a) -> m a b", a=PARITIES),
-        )
         for branch in range(BRANCHES):
             passes("f", branch)
         idle_passes(IDLE_BEHIND_A_GATE)
         for branch in range(BRANCHES):
             activate("f", branch)
-        add_transposed(c_total, written, True, False)
-        kept = keep.tile([P, BRANCHES * H], F32, name="kept")
-        nc.vector.tensor_mul(
-            out=kept[:].rearrange("m (r n) -> m r n", r=BRANCHES),
-            in0=gate_sb["f"][:].rearrange("m (r n) -> m r n", r=BRANCHES),
-            in1=c_old[:].unsqueeze(1).to_broadcast([P, BRANCHES, H]),
-        )
+        add_transposed(c_total[:, 0:H], written)
+        add_transposed(c_total[:, H : 2 * H], gate_sb["f"])
         for branch in range(BRANCHES):
             passes("o", branch)
             activate("o", branch)
-        add_transposed(c_total, kept, False, True)
 
-        tanh_c = keep.tile([P, H], F32, name="tanh_c")
-        nc.scalar.activation(
-            out=tanh_c[:].rearrange("b (m a) -> b m a", a=PARITIES),
-            in_=c_total[:].rearrange("b (a m) -> b m a", a=PARITIES),
-            func=ACT.Tanh,
-        )
+        def rows_of(total):
+            return total.rearrange("b (a m) -> b m a", a=PARITIES)
+
+        def pairs_of(rows):
+            return rows[:].rearrange("b (m a) -> b m a", a=PARITIES)
+
+        kept = keep.tile([P, H], F32, name="kept")
+        nc.vector.tensor_mul(out=pairs_of(kept), in0=rows_of(c_total[:, H : 2 * H]), in1=pairs_of(cl_sb))
         c_rows = keep.tile([P, H], F32, name="c_rows")
-        nc.scalar.copy(
-            out=c_rows[:].rearrange("b (m a) -> b m a", a=PARITIES),
-            in_=c_total[:].rearrange("b (a m) -> b m a", a=PARITIES),
-        )
+        nc.vector.tensor_add(out=pairs_of(c_rows), in0=rows_of(c_total[:, 0:H]), in1=pairs_of(kept))
         nc.sync.dma_start(out=out_1, in_=c_rows[:])
-        add_transposed(o_total, gate_sb["o"], True, True)
+        tanh_c = keep.tile([P, H], F32, name="tanh_c")
+        nc.scalar.activation(out=tanh_c[:], in_=c_rows[:], func=ACT.Tanh)
+        add_transposed(o_total[:], gate_sb["o"])
         h_rows = keep.tile([P, H], F32, name="h_rows")
-        nc.vector.tensor_mul(
-            out=h_rows[:].rearrange("b (m a) -> b m a", a=PARITIES),
-            in0=o_total[:].rearrange("b (a m) -> b m a", a=PARITIES),
-            in1=tanh_c[:].rearrange("b (m a) -> b m a", a=PARITIES),
-        )
+        nc.vector.tensor_mul(out=pairs_of(h_rows), in0=rows_of(o_total[:]), in1=pairs_of(tanh_c))
         nc.sync.dma_start(out=out_0, in_=h_rows[:])

@@ -119,13 +119,12 @@ def tile_customlstmcell_s_kernel(
                     in_=weight_of[gate][branch].rearrange("(m a) k -> m (a k)", a=PARITIES),
                 )
 
-        def load_biases(half):
-            for gate in GATES[2 * half : 2 * half + 2]:
-                for branch in range(BRANCHES):
-                    nc.sync.dma_start(
-                        out=bias[:, slot_of(gate, branch), 0:PARITIES],
-                        in_=bias_of[gate][branch].rearrange("(m a) -> m a", a=PARITIES),
-                    )
+        def load_biases(gate):
+            for branch in range(BRANCHES):
+                nc.sync.dma_start(
+                    out=bias[:, slot_of(gate, branch), 0:PARITIES],
+                    in_=bias_of[gate][branch].rearrange("(m a) -> m a", a=PARITIES),
+                )
 
         nc.sync.dma_start(out=hx_sb[0][:, H:K], in_=y)
         nc.sync.dma_start(out=hx_sb[0][:, 0:H], in_=h_light)
@@ -133,48 +132,37 @@ def tile_customlstmcell_s_kernel(
         nc.vector.tensor_copy(out=hx_sb[1][:, H:K], in_=hx_sb[0][:, H:K])
         load_weights("i")
         load_weights("c")
-        load_biases(0)
+        load_biases("i")
         load_weights("f")
         load_weights("o")
-        load_biases(1)
+        for gate in GATES[1:]:
+            load_biases(gate)
         nc.sync.dma_start(out=cl_sb[:], in_=c_light)
 
         def words(tile_bf16, first_word, step=1):
             return tile_bf16[:].bitcast(F32)[:, first_word : first_word + (P - 1) * step + 1 : step]
 
-        def flip(*sources):
-            bank = flipped.tile([P, 2 * P], F32, name="bank", tag="bank")
-            for u, source in enumerate(sources):
-                nc.tensor.transpose(bank[:, u * P : (u + 1) * P], source, ident[:])
-            return bank
-
-        def quantise(second, bank, codes, scales, name):
-            grouped = keep.tile([P, 4 * P], BF16, name=name, align_bytes=64)
-            src = bank[:].rearrange("q (u r) -> q r u", u=2)
-            dst = grouped[:].bitcast(F32).rearrange("q (r u) -> q r u", u=2)
-            if second:
+        def turn(sources, on_vector):
+            bank = flipped.tile([P, len(sources) * 2 * P], F32, name="bank", tag="bank")
+            for place, (tile_bf16, first_word) in enumerate(sources):
+                for u in range(2):
+                    start = (2 * place + u) * P
+                    nc.tensor.transpose(bank[:, start : start + P], words(tile_bf16, first_word + u, 2), ident[:])
+            grouped = keep.tile([P, len(sources) * 4 * P], BF16, name="grouped", bufs=2 + len(GATES) * BRANCHES, align_bytes=64)
+            src = bank[:].rearrange("q (n u r) -> q n r u", u=2, r=P)
+            dst = grouped[:].bitcast(F32).rearrange("q (n r u) -> q n r u", u=2, r=P)
+            if on_vector:
                 nc.vector.tensor_copy(out=dst, in_=src)
             else:
                 nc.scalar.copy(out=dst, in_=src)
-            return lambda: nc.vector.quantize_mx(out=codes.bitcast(FP8X4), scales=scales, in_=grouped[:])
+            return grouped
 
-        def halves(pair_of_sources, codes, scales, name):
-            pending = []
-            for second, sources in enumerate(pair_of_sources):
-                cols = slice(second * P, (second + 1) * P)
-                bank = flip(*sources)
-                pending.append(quantise(second, bank, codes[:, cols], scales[:, cols], "%s%d" % (name, second)))
-            for issue in pending:
-                issue()
+        def quantise(grouped, codes, scales):
+            nc.vector.quantize_mx(out=codes.bitcast(FP8X4), scales=scales, in_=grouped[:])
 
         hx_codes = keep.tile([P, BRANCHES * P], U32, name="hx_codes", align_bytes=64)
         hx_scales = keep.tile([P, BRANCHES * P], U8, name="hx_scales", align_bytes=64)
-        halves(
-            [(words(hx_sb[branch], 0, 2), words(hx_sb[branch], 1, 2)) for branch in range(BRANCHES)],
-            hx_codes[:],
-            hx_scales[:],
-            "hx_grouped",
-        )
+        hx_grouped = turn([(hx_sb[branch], 0) for branch in range(BRANCHES)], False)
 
         w_codes = keep.tile([P, len(GATES) * BRANCHES, H], U32, name="w_codes", align_bytes=64)
         w_scales = keep.tile([P, len(GATES) * BRANCHES, H], U8, name="w_scales", align_bytes=64)
@@ -183,23 +171,28 @@ def tile_customlstmcell_s_kernel(
             gate_sb[gate] = keep.tile([P, BRANCHES * H], F32, name="gate_%s" % gate)
         z = {}
 
-        def prepare(gate, branch):
-            tile_bf16 = w_sb[gate, branch]
-            slot = slot_of(gate, branch)
-            halves(
-                [(words(tile_bf16, parity * H, 2), words(tile_bf16, parity * H + 1, 2)) for parity in range(PARITIES)],
-                w_codes[:, slot, :],
-                w_scales[:, slot, :],
-                "grouped_%s%d" % (gate, branch),
-            )
+        def prepare(gate):
+            pending = []
+            for branch in range(BRANCHES):
+                slot = slot_of(gate, branch)
+                blocks = [(w_sb[gate, branch], parity * H) for parity in range(PARITIES)]
+                if slot == len(GATES) * BRANCHES - 1:
+                    for parity in range(PARITIES):
+                        pending.append((turn(blocks[parity : parity + 1], parity == 1), slot, parity * P, P))
+                else:
+                    pending.append((turn(blocks, branch == 1), slot, 0, H))
+            for grouped, slot, first, width in pending:
+                cols = slice(first, first + width)
+                quantise(grouped, w_codes[:, slot, cols], w_scales[:, slot, cols])
 
         def passes(gate, branch):
             slot = slot_of(gate, branch)
-            z[gate, branch] = sums.tile([P, H], F32, name="z", tag="z")
+            if branch == 0:
+                z[gate] = sums.tile([P, BRANCHES * H], F32, name="z", tag="z")
             for parity in range(PARITIES):
                 cols = slice(parity * P, (parity + 1) * P)
                 nc.tensor.matmul_mx(
-                    out=z[gate, branch][:, cols],
+                    out=z[gate][:, branch * H + parity * P : branch * H + (parity + 1) * P],
                     lhsT=w_codes[:, slot, cols].bitcast(FP8X4),
                     lhsT_scale=w_scales[:, slot, cols],
                     rhs=hx_codes[:, branch * P : (branch + 1) * P].bitcast(FP8X4),
@@ -210,9 +203,10 @@ def tile_customlstmcell_s_kernel(
 
         def activate(gate, branch):
             for parity in range(PARITIES):
+                cols = slice(branch * H + parity * P, branch * H + (parity + 1) * P)
                 nc.scalar.activation(
-                    out=gate_sb[gate][:, branch * H + parity * P : branch * H + (parity + 1) * P],
-                    in_=z[gate, branch][:, parity * P : (parity + 1) * P],
+                    out=gate_sb[gate][:, cols],
+                    in_=z[gate][:, cols],
                     func=GATE_FUNC[gate],
                     bias=bias[:, slot_of(gate, branch), parity : parity + 1],
                 )
@@ -229,29 +223,26 @@ def tile_customlstmcell_s_kernel(
                         is_transpose=True,
                     )
 
-        for branch in range(BRANCHES):
-            prepare("i", branch)
+        quantise(hx_grouped, hx_codes[:], hx_scales[:])
+        prepare("i")
         idle_passes(IDLE_ALONE)
-        for branch in range(BRANCHES):
-            prepare("c", branch)
+        prepare("c")
         for branch in range(BRANCHES):
             passes("i", branch)
         idle_passes(IDLE_BEHIND_A_GATE)
         for branch in range(BRANCHES):
             activate("i", branch)
 
-        for branch in range(BRANCHES):
-            prepare("f", branch)
+        prepare("f")
         for branch in range(BRANCHES):
             passes("c", branch)
         idle_passes(IDLE_BEHIND_A_GATE)
         for branch in range(BRANCHES):
             activate("c", branch)
 
-        prepare("o", 0)
         written = keep.tile([P, BRANCHES * H], F32, name="written")
         nc.vector.tensor_mul(out=written[:], in0=gate_sb["i"][:], in1=gate_sb["c"][:])
-        prepare("o", 1)
+        prepare("o")
         for branch in range(BRANCHES):
             passes("f", branch)
         idle_passes(IDLE_BEHIND_A_GATE)
@@ -261,6 +252,7 @@ def tile_customlstmcell_s_kernel(
         add_transposed(c_total[:, H : 2 * H], gate_sb["f"])
         for branch in range(BRANCHES):
             passes("o", branch)
+        for branch in range(BRANCHES):
             activate("o", branch)
 
         def rows_of(total):

@@ -71,7 +71,7 @@ def tile_customlstmcell_s_kernel(
         totals = ctx.enter_context(tc.psum_pool(name="totals", bufs=1))
         ctx.enter_context(tc.manual_schedule())
 
-        c_total = totals.tile([P, 2 * H], F32, name="c_total")
+        c_total = totals.tile([P, H], F32, name="c_total")
         o_total = totals.tile([P, H], F32, name="o_total")
         zeros = keep.tile([P, 4 * P], BF16, name="zeros", align_bytes=64)
         zero_codes = keep.tile([P, P], U32, name="zero_codes", align_bytes=64)
@@ -131,13 +131,13 @@ def tile_customlstmcell_s_kernel(
         nc.sync.dma_start(out=hx_sb[1][:, 0:H], in_=h_temp)
         nc.vector.tensor_copy(out=hx_sb[1][:, H:K], in_=hx_sb[0][:, H:K])
         load_weights("i")
+        nc.sync.dma_start(out=cl_sb[:], in_=c_light)
         load_weights("c")
         load_biases("i")
         load_weights("f")
         load_weights("o")
         for gate in GATES[1:]:
             load_biases(gate)
-        nc.sync.dma_start(out=cl_sb[:], in_=c_light)
 
         def words(tile_bf16, first_word, step=1):
             return tile_bf16[:].bitcast(F32)[:, first_word : first_word + (P - 1) * step + 1 : step]
@@ -162,7 +162,7 @@ def tile_customlstmcell_s_kernel(
 
         hx_codes = keep.tile([P, BRANCHES * P], U32, name="hx_codes", align_bytes=64)
         hx_scales = keep.tile([P, BRANCHES * P], U8, name="hx_scales", align_bytes=64)
-        hx_grouped = turn([(hx_sb[branch], 0) for branch in range(BRANCHES)], False)
+        hx_grouped = turn([(hx_sb[branch], 0) for branch in range(BRANCHES)], True)
 
         w_codes = keep.tile([P, len(GATES) * BRANCHES, H], U32, name="w_codes", align_bytes=64)
         w_scales = keep.tile([P, len(GATES) * BRANCHES, H], U8, name="w_scales", align_bytes=64)
@@ -180,19 +180,21 @@ def tile_customlstmcell_s_kernel(
                     for parity in range(PARITIES):
                         pending.append((turn(blocks[parity : parity + 1], parity == 1), slot, parity * P, P))
                 else:
-                    pending.append((turn(blocks, branch == 1), slot, 0, H))
+                    pending.append((turn(blocks, branch == 1 and gate != "i"), slot, 0, H))
             for grouped, slot, first, width in pending:
                 cols = slice(first, first + width)
                 quantise(grouped, w_codes[:, slot, cols], w_scales[:, slot, cols])
 
         def passes(gate, branch):
             slot = slot_of(gate, branch)
-            if branch == 0:
-                z[gate] = sums.tile([P, BRANCHES * H], F32, name="z", tag="z")
+            if gate == GATES[-1]:
+                z[gate, branch] = flipped.tile([P, H], F32, name="z_last", tag="bank")
+            else:
+                z[gate, branch] = sums.tile([P, H], F32, name="z", tag="z")
             for parity in range(PARITIES):
                 cols = slice(parity * P, (parity + 1) * P)
                 nc.tensor.matmul_mx(
-                    out=z[gate][:, branch * H + parity * P : branch * H + (parity + 1) * P],
+                    out=z[gate, branch][:, cols],
                     lhsT=w_codes[:, slot, cols].bitcast(FP8X4),
                     lhsT_scale=w_scales[:, slot, cols],
                     rhs=hx_codes[:, branch * P : (branch + 1) * P].bitcast(FP8X4),
@@ -203,29 +205,39 @@ def tile_customlstmcell_s_kernel(
 
         def activate(gate, branch):
             for parity in range(PARITIES):
-                cols = slice(branch * H + parity * P, branch * H + (parity + 1) * P)
                 nc.scalar.activation(
-                    out=gate_sb[gate][:, cols],
-                    in_=z[gate][:, cols],
+                    out=gate_sb[gate][:, branch * H + parity * P : branch * H + (parity + 1) * P],
+                    in_=z[gate, branch][:, parity * P : (parity + 1) * P],
                     func=GATE_FUNC[gate],
                     bias=bias[:, slot_of(gate, branch), parity : parity + 1],
                 )
 
-        def add_transposed(total, terms):
+        def add_transposed(total, terms, first, last):
             for branch in range(BRANCHES):
                 for parity in range(PARITIES):
                     nc.tensor.matmul(
                         out=total[:, parity * P : (parity + 1) * P],
                         lhsT=terms[:, branch * H + parity * P : branch * H + (parity + 1) * P],
                         rhs=ident[:],
-                        start=branch == 0 and parity == 0,
-                        stop=branch == BRANCHES - 1 and parity == PARITIES - 1,
+                        start=first and branch == 0 and parity == 0,
+                        stop=last and branch == BRANCHES - 1 and parity == PARITIES - 1,
                         is_transpose=True,
                     )
+
+        def turn_c_light():
+            bank = flipped.tile([P, P], F32, name="cl_bank", tag="bank")
+            nc.tensor.transpose(bank[:], words(cl_sb, 0), ident[:])
+            c_old = keep.tile([P, H], F32, name="c_old")
+            nc.vector.tensor_copy(
+                out=c_old[:].rearrange("m (a b) -> m a b", a=PARITIES),
+                in_=bank[:].bitcast(BF16).rearrange("m (b a) -> m a b", a=PARITIES),
+            )
+            return c_old
 
         quantise(hx_grouped, hx_codes[:], hx_scales[:])
         prepare("i")
         idle_passes(IDLE_ALONE)
+        c_old = turn_c_light()
         prepare("c")
         for branch in range(BRANCHES):
             passes("i", branch)
@@ -248,27 +260,29 @@ def tile_customlstmcell_s_kernel(
         idle_passes(IDLE_BEHIND_A_GATE)
         for branch in range(BRANCHES):
             activate("f", branch)
-        add_transposed(c_total[:, 0:H], written)
-        add_transposed(c_total[:, H : 2 * H], gate_sb["f"])
+        add_transposed(c_total, written, True, False)
+        kept = keep.tile([P, BRANCHES * H], F32, name="kept")
+        for branch in range(BRANCHES):
+            cols = slice(branch * H, (branch + 1) * H)
+            nc.vector.tensor_mul(out=kept[:, cols], in0=gate_sb["f"][:, cols], in1=c_old[:])
         for branch in range(BRANCHES):
             passes("o", branch)
         for branch in range(BRANCHES):
             activate("o", branch)
+        add_transposed(c_total, kept, False, True)
 
         def rows_of(total):
-            return total.rearrange("b (a m) -> b m a", a=PARITIES)
+            return total[:].rearrange("b (a m) -> b m a", a=PARITIES)
 
         def pairs_of(rows):
             return rows[:].rearrange("b (m a) -> b m a", a=PARITIES)
 
-        kept = keep.tile([P, H], F32, name="kept")
-        nc.vector.tensor_mul(out=pairs_of(kept), in0=rows_of(c_total[:, H : 2 * H]), in1=pairs_of(cl_sb))
-        c_rows = keep.tile([P, H], F32, name="c_rows")
-        nc.vector.tensor_add(out=pairs_of(c_rows), in0=rows_of(c_total[:, 0:H]), in1=pairs_of(kept))
-        nc.sync.dma_start(out=out_1, in_=c_rows[:])
         tanh_c = keep.tile([P, H], F32, name="tanh_c")
-        nc.scalar.activation(out=tanh_c[:], in_=c_rows[:], func=ACT.Tanh)
-        add_transposed(o_total[:], gate_sb["o"])
+        nc.scalar.activation(out=pairs_of(tanh_c), in_=rows_of(c_total), func=ACT.Tanh)
+        c_rows = keep.tile([P, H], F32, name="c_rows")
+        nc.scalar.copy(out=pairs_of(c_rows), in_=rows_of(c_total))
+        nc.sync.dma_start(out=out_1, in_=c_rows[:])
+        add_transposed(o_total, gate_sb["o"], True, True)
         h_rows = keep.tile([P, H], F32, name="h_rows")
-        nc.vector.tensor_mul(out=pairs_of(h_rows), in0=rows_of(o_total[:]), in1=pairs_of(tanh_c))
+        nc.vector.tensor_mul(out=pairs_of(h_rows), in0=rows_of(o_total), in1=pairs_of(tanh_c))
         nc.sync.dma_start(out=out_0, in_=h_rows[:])

@@ -16,8 +16,6 @@ K = 2 * H
 BRANCHES = 2
 PARITIES = 2
 IDLE_AT_START = 10
-IDLE_ALONE = 6
-IDLE_BEHIND_A_GATE = 2
 GATES = ("i", "c", "f", "o")
 GATE_FUNC = {"i": ACT.Sigmoid, "c": ACT.Tanh, "f": ACT.Sigmoid, "o": ACT.Sigmoid}
 
@@ -236,19 +234,16 @@ def tile_customlstmcell_s_kernel(
 
         quantise(hx_grouped, hx_codes[:], hx_scales[:])
         prepare("i")
-        idle_passes(IDLE_ALONE)
         c_old = turn_c_light()
         prepare("c")
         for branch in range(BRANCHES):
             passes("i", branch)
-        idle_passes(IDLE_BEHIND_A_GATE)
         for branch in range(BRANCHES):
             activate("i", branch)
 
         prepare("f")
         for branch in range(BRANCHES):
             passes("c", branch)
-        idle_passes(IDLE_BEHIND_A_GATE)
         for branch in range(BRANCHES):
             activate("c", branch)
 
@@ -257,7 +252,6 @@ def tile_customlstmcell_s_kernel(
         prepare("o")
         for branch in range(BRANCHES):
             passes("f", branch)
-        idle_passes(IDLE_BEHIND_A_GATE)
         for branch in range(BRANCHES):
             activate("f", branch)
         add_transposed(c_total, written, True, False)

@@ -15,6 +15,7 @@ H = 256
 K = 2 * H
 BRANCHES = 2
 PARITIES = 2
+PLAIN_AT_START = 5
 IDLE_AT_START = 10
 GATES = ("i", "c", "f", "o")
 GATE_FUNC = {"i": ACT.Sigmoid, "c": ACT.Tanh, "f": ACT.Sigmoid, "o": ACT.Sigmoid}
@@ -74,7 +75,9 @@ def tile_customlstmcell_s_kernel(
         zeros = keep.tile([P, 4 * P], BF16, name="zeros", align_bytes=64)
         zero_codes = keep.tile([P, P], U32, name="zero_codes", align_bytes=64)
         zero_scales = keep.tile([P, P], U8, name="zero_scales", align_bytes=64)
-        nc.vector.memset(zeros[:], 0.0)
+        plain_zeros = keep.tile([P, P], BF16, name="plain_zeros")
+        nc.vector.memset(plain_zeros[:], 0.0)
+        nc.vector.memset(zeros[:].bitcast(U32), 0)
         nc.vector.quantize_mx(out=zero_codes[:].bitcast(FP8X4), scales=zero_scales[:], in_=zeros[:])
 
         def idle_passes(count):
@@ -89,6 +92,8 @@ def tile_customlstmcell_s_kernel(
                     stop=True,
                 )
 
+        for repeat in range(PLAIN_AT_START):
+            nc.tensor.matmul(out=o_total[:, 0:P], lhsT=plain_zeros[:], rhs=plain_zeros[:], start=True, stop=True)
         idle_passes(IDLE_AT_START)
 
         ident = keep.tile([P, P], F32, name="ident")

@@ -16,7 +16,7 @@ K = 2 * H
 BRANCHES = 2
 PARITIES = 2
 PLAIN_AT_START = 5
-IDLE_AT_START = 10
+IDLE_AT_START = 6
 GATES = ("i", "c", "f", "o")
 GATE_FUNC = {"i": ACT.Sigmoid, "c": ACT.Tanh, "f": ACT.Sigmoid, "o": ACT.Sigmoid}
 

from contextlib import ExitStack

import concourse.mybir as mybir
from concourse.masks import make_identity

BF16 = mybir.dt.bfloat16
F32 = mybir.dt.float32
U32 = mybir.dt.uint32
U8 = mybir.dt.uint8
FP8X4 = mybir.dt.float8_e4m3fn_x4
ACT = mybir.ActivationFunctionType

P = 128
H = 256
K = 2 * H
BRANCHES = 2
PARITIES = 2
PLAIN_AT_START = 5
IDLE_AT_START = 6
GATES = ("i", "c", "f", "o")
GATE_FUNC = {"i": ACT.Sigmoid, "c": ACT.Tanh, "f": ACT.Sigmoid, "o": ACT.Sigmoid}

FLOPS = 2 * P * K * len(GATES) * BRANCHES * H


def tile_customlstmcell_s_kernel(
    tc,
    y,
    h_light,
    c_light,
    h_temp,
    c_temp,
    w_f_light,
    b_f_light,
    w_i_light,
    b_i_light,
    w_c_light,
    b_c_light,
    w_o_light,
    b_o_light,
    w_f_light_temp,
    b_f_light_temp,
    w_i_light_temp,
    b_i_light_temp,
    w_c_light_temp,
    b_c_light_temp,
    w_o_light_temp,
    b_o_light_temp,
    out_0,
    out_1,
):
    nc = tc.nc
    weight_of = {
        "f": (w_f_light, w_f_light_temp),
        "i": (w_i_light, w_i_light_temp),
        "c": (w_c_light, w_c_light_temp),
        "o": (w_o_light, w_o_light_temp),
    }
    bias_of = {
        "f": (b_f_light, b_f_light_temp),
        "i": (b_i_light, b_i_light_temp),
        "c": (b_c_light, b_c_light_temp),
        "o": (b_o_light, b_o_light_temp),
    }

    with ExitStack() as ctx:
        keep = ctx.enter_context(tc.tile_pool(name="keep", bufs=1))
        flipped = ctx.enter_context(tc.psum_pool(name="flipped", bufs=4))
        sums = ctx.enter_context(tc.psum_pool(name="sums", bufs=2))
        totals = ctx.enter_context(tc.psum_pool(name="totals", bufs=1))
        ctx.enter_context(tc.manual_schedule())

        c_total = totals.tile([P, H], F32, name="c_total")
        o_total = totals.tile([P, H], F32, name="o_total")
        zeros = keep.tile([P, 4 * P], BF16, name="zeros", align_bytes=64)
        zero_codes = keep.tile([P, P], U32, name="zero_codes", align_bytes=64)
        zero_scales = keep.tile([P, P], U8, name="zero_scales", align_bytes=64)
        plain_zeros = keep.tile([P, P], BF16, name="plain_zeros")
        nc.vector.memset(plain_zeros[:], 0.0)
        nc.vector.memset(zeros[:].bitcast(U32), 0)
        nc.vector.quantize_mx(out=zero_codes[:].bitcast(FP8X4), scales=zero_scales[:], in_=zeros[:])

        def idle_passes(count):
            for repeat in range(count):
                nc.tensor.matmul_mx(
                    out=o_total[:, 0:P],
                    lhsT=zero_codes[:].bitcast(FP8X4),
                    lhsT_scale=zero_scales[:],
                    rhs=zero_codes[:].bitcast(FP8X4),
                    rhs_scale=zero_scales[:],
                    start=True,
                    stop=True,
                )

        for repeat in range(PLAIN_AT_START):
            nc.tensor.matmul(out=o_total[:, 0:P], lhsT=plain_zeros[:], rhs=plain_zeros[:], start=True, stop=True)
        idle_passes(IDLE_AT_START)

        ident = keep.tile([P, P], F32, name="ident")
        make_identity(nc, ident[:])
        warm_in = keep.tile([P, 1], F32, name="warm_in")
        warm_out = keep.tile([P, 1], F32, name="warm_out")
        nc.vector.memset(warm_in[:], 0.0)
        nc.scalar.activation(out=warm_out[:], in_=warm_in[:], func=ACT.Sigmoid)

        hx_sb = [keep.tile([P, K], BF16, name="hx_sb%d" % branch) for branch in range(BRANCHES)]
        cl_sb = keep.tile([P, H], BF16, name="cl_sb")
        w_sb = {}
        for gate in GATES:
            for branch in range(BRANCHES):
                w_sb[gate, branch] = keep.tile([P, PARITIES * K], BF16, name="w_%s%d" % (gate, branch))

        bias = keep.tile([P, len(GATES) * BRANCHES, 16], BF16, name="bias")

        def slot_of(gate, branch):
            return BRANCHES * GATES.index(gate) + branch

        def load_weights(gate):
            for branch in range(BRANCHES):
                nc.sync.dma_start(
                    out=w_sb[gate, branch][:],
                    in_=weight_of[gate][branch].rearrange("(m a) k -> m (a k)", a=PARITIES),
                )

        def load_biases(gate):
            for branch in range(BRANCHES):
                nc.sync.dma_start(
                    out=bias[:, slot_of(gate, branch), 0:PARITIES],
                    in_=bias_of[gate][branch].rearrange("(m a) -> m a", a=PARITIES),
                )

        nc.sync.dma_start(out=hx_sb[0][:, H:K], in_=y)
        nc.sync.dma_start(out=hx_sb[0][:, 0:H], in_=h_light)
        nc.sync.dma_start(out=hx_sb[1][:, 0:H], in_=h_temp)
        nc.vector.tensor_copy(out=hx_sb[1][:, H:K], in_=hx_sb[0][:, H:K])
        load_weights("i")
        nc.sync.dma_start(out=cl_sb[:], in_=c_light)
        load_weights("c")
        load_biases("i")
        load_weights("f")
        load_weights("o")
        for gate in GATES[1:]:
            load_biases(gate)

        def words(tile_bf16, first_word, step=1):
            return tile_bf16[:].bitcast(F32)[:, first_word : first_word + (P - 1) * step + 1 : step]

        def turn(sources, on_vector):
            bank = flipped.tile([P, len(sources) * 2 * P], F32, name="bank", tag="bank")
            for place, (tile_bf16, first_word) in enumerate(sources):
                for u in range(2):
                    start = (2 * place + u) * P
                    nc.tensor.transpose(bank[:, start : start + P], words(tile_bf16, first_word + u, 2), ident[:])
            grouped = keep.tile([P, len(sources) * 4 * P], BF16, name="grouped", bufs=2 + len(GATES) * BRANCHES, align_bytes=64)
            src = bank[:].rearrange("q (n u r) -> q n r u", u=2, r=P)
            dst = grouped[:].bitcast(F32).rearrange("q (n r u) -> q n r u", u=2, r=P)
            if on_vector:
                nc.vector.tensor_copy(out=dst, in_=src)
            else:
                nc.scalar.copy(out=dst, in_=src)
            return grouped

        def quantise(grouped, codes, scales):
            nc.vector.quantize_mx(out=codes.bitcast(FP8X4), scales=scales, in_=grouped[:])

        hx_codes = keep.tile([P, BRANCHES * P], U32, name="hx_codes", align_bytes=64)
        hx_scales = keep.tile([P, BRANCHES * P], U8, name="hx_scales", align_bytes=64)
        hx_grouped = turn([(hx_sb[branch], 0) for branch in range(BRANCHES)], True)

        w_codes = keep.tile([P, len(GATES) * BRANCHES, H], U32, name="w_codes", align_bytes=64)
        w_scales = keep.tile([P, len(GATES) * BRANCHES, H], U8, name="w_scales", align_bytes=64)
        gate_sb = {}
        for gate in GATES:
            gate_sb[gate] = keep.tile([P, BRANCHES * H], F32, name="gate_%s" % gate)
        z = {}

        def prepare(gate):
            pending = []
            for branch in range(BRANCHES):
                slot = slot_of(gate, branch)
                blocks = [(w_sb[gate, branch], parity * H) for parity in range(PARITIES)]
                if slot == len(GATES) * BRANCHES - 1:
                    for parity in range(PARITIES):
                        pending.append((turn(blocks[parity : parity + 1], parity == 1), slot, parity * P, P))
                else:
                    pending.append((turn(blocks, branch == 1 and gate != "i"), slot, 0, H))
            for grouped, slot, first, width in pending:
                cols = slice(first, first + width)
                quantise(grouped, w_codes[:, slot, cols], w_scales[:, slot, cols])

        def passes(gate, branch):
            slot = slot_of(gate, branch)
            if gate == GATES[-1]:
                z[gate, branch] = flipped.tile([P, H], F32, name="z_last", tag="bank")
            else:
                z[gate, branch] = sums.tile([P, H], F32, name="z", tag="z")
            for parity in range(PARITIES):
                cols = slice(parity * P, (parity + 1) * P)
                nc.tensor.matmul_mx(
                    out=z[gate, branch][:, cols],
                    lhsT=w_codes[:, slot, cols].bitcast(FP8X4),
                    lhsT_scale=w_scales[:, slot, cols],
                    rhs=hx_codes[:, branch * P : (branch + 1) * P].bitcast(FP8X4),
                    rhs_scale=hx_scales[:, branch * P : (branch + 1) * P],
                    start=True,
                    stop=True,
                )

        def activate(gate, branch):
            for parity in range(PARITIES):
                nc.scalar.activation(
                    out=gate_sb[gate][:, branch * H + parity * P : branch * H + (parity + 1) * P],
                    in_=z[gate, branch][:, parity * P : (parity + 1) * P],
                    func=GATE_FUNC[gate],
                    bias=bias[:, slot_of(gate, branch), parity : parity + 1],
                )

        def add_transposed(total, terms, first, last):
            for branch in range(BRANCHES):
                for parity in range(PARITIES):
                    nc.tensor.matmul(
                        out=total[:, parity * P : (parity + 1) * P],
                        lhsT=terms[:, branch * H + parity * P : branch * H + (parity + 1) * P],
                        rhs=ident[:],
                        start=first and branch == 0 and parity == 0,
                        stop=last and branch == BRANCHES - 1 and parity == PARITIES - 1,
                        is_transpose=True,
                    )

        def turn_c_light():
            bank = flipped.tile([P, P], F32, name="cl_bank", tag="bank")
            nc.tensor.transpose(bank[:], words(cl_sb, 0), ident[:])
            c_old = keep.tile([P, H], F32, name="c_old")
            nc.vector.tensor_copy(
                out=c_old[:].rearrange("m (a b) -> m a b", a=PARITIES),
                in_=bank[:].bitcast(BF16).rearrange("m (b a) -> m a b", a=PARITIES),
            )
            return c_old

        quantise(hx_grouped, hx_codes[:], hx_scales[:])
        prepare("i")
        c_old = turn_c_light()
        prepare("c")
        for branch in range(BRANCHES):
            passes("i", branch)
        for branch in range(BRANCHES):
            activate("i", branch)

        prepare("f")
        for branch in range(BRANCHES):
            passes("c", branch)
        for branch in range(BRANCHES):
            activate("c", branch)

        written = keep.tile([P, BRANCHES * H], F32, name="written")
        nc.vector.tensor_mul(out=written[:], in0=gate_sb["i"][:], in1=gate_sb["c"][:])
        prepare("o")
        for branch in range(BRANCHES):
            passes("f", branch)
        for branch in range(BRANCHES):
            activate("f", branch)
        add_transposed(c_total, written, True, False)
        kept = keep.tile([P, BRANCHES * H], F32, name="kept")
        for branch in range(BRANCHES):
            cols = slice(branch * H, (branch + 1) * H)
            nc.vector.tensor_mul(out=kept[:, cols], in0=gate_sb["f"][:, cols], in1=c_old[:])
        for branch in range(BRANCHES):
            passes("o", branch)
        for branch in range(BRANCHES):
            activate("o", branch)
        add_transposed(c_total, kept, False, True)

        def rows_of(total):
            return total[:].rearrange("b (a m) -> b m a", a=PARITIES)

        def pairs_of(rows):
            return rows[:].rearrange("b (m a) -> b m a", a=PARITIES)

        tanh_c = keep.tile([P, H], F32, name="tanh_c")
        nc.scalar.activation(out=pairs_of(tanh_c), in_=rows_of(c_total), func=ACT.Tanh)
        c_rows = keep.tile([P, H], F32, name="c_rows")
        nc.scalar.copy(out=pairs_of(c_rows), in_=rows_of(c_total))
        nc.sync.dma_start(out=out_1, in_=c_rows[:])
        add_transposed(o_total, gate_sb["o"], True, True)
        h_rows = keep.tile([P, H], F32, name="h_rows")
        nc.vector.tensor_mul(out=pairs_of(h_rows), in0=rows_of(o_total), in1=pairs_of(tanh_c))
        nc.sync.dma_start(out=out_0, in_=h_rows[:])
